import numpy as np
import ml_dtypes

BF16 = ml_dtypes.bfloat16


def bf(x):
    return np.asarray(x, np.float32).astype(BF16)


def f32(x):
    return np.asarray(x, np.float32)


def f64(x):
    return np.asarray(x).astype(np.float64)


def striped(idx):
    return np.tile(idx.reshape(-1, 16).T, (8, 1))


C, H, S, N = 384, 768, 4096, 2048


def silu(v):
    return v / (1.0 + np.exp(-v))


def setup_inputs():
    return {
        "base": f32(np.random.standard_normal((C, S))),
        "h": f32(np.random.standard_normal((C, N))),
        "w1": bf(np.random.standard_normal((C, H)) / np.sqrt(C)),
        "b1": f32(0.2 * np.random.standard_normal((H, 1))),
        "w2": bf(np.random.standard_normal((H, H)) / np.sqrt(H)),
        "b2": f32(0.2 * np.random.standard_normal((H, 1))),
        "w3": bf(np.random.standard_normal((H, C)) / np.sqrt(H)),
        "b3": f32(0.2 * np.random.standard_normal((C, 1))),
        "offs": striped(np.random.permutation(S)[:N]),
    }


def reference(base, h, w1, b1, w2, b2, w3, b3, offs):
    idx = offs[:16].T.reshape(-1)
    u = f64(w1).T @ f64(h) + f64(b1)
    a = silu(u)
    t = f64(w2).T @ a + f64(b2)
    y = f64(w3).T @ t + f64(b3)
    out = f64(base).copy()
    out[:, idx] = y + f64(h)
    return out

@@ -1,0 +1,118 @@
+import concourse.mybir as mybir
+from concourse.masks import make_identity
+
+BF16 = mybir.dt.bfloat16
+F32 = mybir.dt.float32
+U16 = mybir.dt.uint16
+ADD = mybir.AluOpType.add
+SILU = mybir.ActivationFunctionType.Silu
+IDENTITY = mybir.ActivationFunctionType.Identity
+
+P = 128
+C, H, S, N = 384, 768, 4096, 2048
+CB = C // P
+HB = H // P
+TOK = 512
+NT = N // TOK
+FLOPS = 2 * N * (C * H + H * H + H * C)
+
+
+def block(i):
+    return slice(i * P, (i + 1) * P)
+
+
+def chunk(n):
+    return slice(n * TOK, (n + 1) * TOK)
+
+
+def linear(nc, psum, weights, moving, out_block, n):
+    acc = psum.tile([P, TOK], F32, name="acc")
+    last = len(moving) - 1
+    for k, rows in enumerate(moving):
+        nc.tensor.matmul(
+            acc[:], weights[:, k, block(out_block)], rows[:, chunk(n)], start=(k == 0), stop=(k == last)
+        )
+    return acc
+
+
+def tile_kanex_b_kernel(tc, base, h, w1, b1, w2, b2, w3, b3, offs, out):
+    nc = tc.nc
+    with (
+        tc.tile_pool(name="held", bufs=1) as held,
+        tc.psum_pool(name="psum", bufs=8) as psum,
+    ):
+        offsets = held.tile([P, N // 16], U16, name="offsets")
+        nc.sync.dma_start(offsets[:], offs)
+
+        bias_rows = held.tile([P, P], F32, name="bias_rows")
+        nc.vector.memset(bias_rows[:], 0.0)
+        first_row = {}
+        rows_used = 0
+        for name, vector in (("b1", b1), ("b2", b2), ("b3", b3)):
+            rows = vector.shape[0] // P
+            first_row[name] = rows_used
+            nc.scalar.dma_start(
+                bias_rows[rows_used : rows_used + rows, :], vector.rearrange("(m p) o -> m (p o)", p=P)
+            )
+            rows_used += rows
+
+        w1_sb = held.tile([P, CB, H], BF16, name="w1_sb")
+        nc.sync.dma_start(w1_sb[:], w1.rearrange("(k p) m -> p k m", p=P))
+        h_f32 = [held.tile([P, N], F32, name=f"h_f32_{c}") for c in range(CB)]
+        for n in range(NT):
+            for c in range(CB):
+                nc.sync.dma_start(h_f32[c][:, chunk(n)], h[block(c), chunk(n)])
+            if n == 1:
+                w2_sb = held.tile([P, HB, H], BF16, name="w2_sb")
+                nc.sync.dma_start(w2_sb[:], w2.rearrange("(k p) m -> p k m", p=P))
+        w3_sb = held.tile([P, HB, C], BF16, name="w3_sb")
+        nc.sync.dma_start(w3_sb[:], w3.rearrange("(k p) m -> p k m", p=P))
+        window = [held.tile([P, S], F32, name=f"window_{c}") for c in range(CB)]
+        for c in range(CB):
+            nc.sync.dma_start(window[c][:], base[block(c), :])
+
+        identity = held.tile([P, P], F32, name="identity")
+        make_identity(nc, identity[:])
+        flipped = psum.tile([P, TOK], F32, name="acc")
+        nc.tensor.transpose(flipped[:, :P], bias_rows[:], identity[:])
+        bias = held.tile([P, rows_used], F32, name="bias")
+        nc.vector.tensor_copy(bias[:], flipped[:, :rows_used])
+
+        def bias_column(name, i):
+            j = first_row[name] + i
+            return bias[:, j : j + 1]
+
+        h_bf = [held.tile([P, N], BF16, name=f"h_bf_{c}") for c in range(CB)]
+        for n in range(NT):
+            for c in range(CB):
+                nc.vector.tensor_copy(h_bf[c][:, chunk(n)], h_f32[c][:, chunk(n)])
+
+        a_bf = [held.tile([P, N], BF16, name=f"a_bf_{m}") for m in range(HB)]
+        t_bf = [held.tile([P, N], BF16, name=f"t_bf_{m}") for m in range(HB)]
+        y = [held.tile([P, N], F32, name=f"y_{c}") for c in range(CB)]
+
+        def layer1(n):
+            for m in range(HB):
+                acc = linear(nc, psum, w1_sb, h_bf, m, n)
+                nc.scalar.activation(a_bf[m][:, chunk(n)], acc[:], SILU, bias=bias_column("b1", m))
+
+        def layer2(n):
+            for m in range(HB):
+                acc = linear(nc, psum, w2_sb, a_bf, m, n)
+                nc.vector.tensor_scalar_add(t_bf[m][:, chunk(n)], acc[:], bias_column("b2", m))
+
+        def layer3(c, n):
+            acc = linear(nc, psum, w3_sb, t_bf, c, n)
+            nc.scalar.activation(y[c][:, chunk(n)], acc[:], IDENTITY, bias=bias_column("b3", c))
+
+        layer1(0)
+        for n in range(NT):
+            if n + 1 < NT:
+                layer1(n + 1)
+            layer2(n)
+
+        for c in range(CB):
+            for n in range(NT):
+                layer3(c, n)
+            nc.vector.tensor_tensor(window[c][:].indirect(offsets[:]), y[c][:], h_f32[c][:], ADD)
+            nc.sync.dma_start(out[block(c), :], window[c][:])

@@ -14,6 +14,7 @@ CB = C // P
 HB = H // P
 TOK = 512
 NT = N // TOK
+SIDE = 3
 FLOPS = 2 * N * (C * H + H * H + H * C)
 
 
@@ -41,8 +42,11 @@ def tile_kanex_b_kernel(tc, base, h, w1, b1, w2, b2, w3, b3, offs, out):
         tc.tile_pool(name="held", bufs=1) as held,
         tc.psum_pool(name="psum", bufs=8) as psum,
     ):
-        offsets = held.tile([P, N // 16], U16, name="offsets")
-        nc.sync.dma_start(offsets[:], offs)
+        w1_sb = held.tile([P, CB, H], BF16, name="w1_sb")
+        h_f32 = [held.tile([P, N], F32, name=f"h_f32_{c}") for c in range(CB)]
+        for k in range(CB):
+            nc.scalar.dma_start(w1_sb[:, k, :], w1[block(k), :])
+            nc.sync.dma_start(h_f32[k][:, chunk(0)], h[block(k), chunk(0)])
 
         bias_rows = held.tile([P, P], F32, name="bias_rows")
         nc.vector.memset(bias_rows[:], 0.0)
@@ -56,20 +60,30 @@ def tile_kanex_b_kernel(tc, base, h, w1, b1, w2, b2, w3, b3, offs, out):
             )
             rows_used += rows
 
-        w1_sb = held.tile([P, CB, H], BF16, name="w1_sb")
-        nc.sync.dma_start(w1_sb[:], w1.rearrange("(k p) m -> p k m", p=P))
-        h_f32 = [held.tile([P, N], F32, name=f"h_f32_{c}") for c in range(CB)]
-        for n in range(NT):
+        def load_h(n):
             for c in range(CB):
                 nc.sync.dma_start(h_f32[c][:, chunk(n)], h[block(c), chunk(n)])
-            if n == 1:
-                w2_sb = held.tile([P, HB, H], BF16, name="w2_sb")
-                nc.sync.dma_start(w2_sb[:], w2.rearrange("(k p) m -> p k m", p=P))
+
+        load_h(1)
+        w2_sb = held.tile([P, HB, H], BF16, name="w2_sb")
+        nc.sync.dma_start(w2_sb[:], w2.rearrange("(k p) m -> p k m", p=P))
+        load_h(2)
+        load_h(3)
         w3_sb = held.tile([P, HB, C], BF16, name="w3_sb")
         nc.sync.dma_start(w3_sb[:], w3.rearrange("(k p) m -> p k m", p=P))
+        offsets = held.tile([P, N // 16], U16, name="offsets")
+        nc.sync.dma_start(offsets[:], offs)
         window = [held.tile([P, S], F32, name=f"window_{c}") for c in range(CB)]
         for c in range(CB):
             nc.sync.dma_start(window[c][:], base[block(c), :])
+
+        h_bf = [held.tile([P, N], BF16, name=f"h_bf_{c}") for c in range(CB)]
+
+        def round_h(n):
+            for c in range(CB):
+                nc.vector.tensor_copy(h_bf[c][:, chunk(n)], h_f32[c][:, chunk(n)])
+
+        round_h(0)
 
         identity = held.tile([P, P], F32, name="identity")
         make_identity(nc, identity[:])
@@ -82,19 +96,23 @@ def tile_kanex_b_kernel(tc, base, h, w1, b1, w2, b2, w3, b3, offs, out):
             j = first_row[name] + i
             return bias[:, j : j + 1]
 
-        h_bf = [held.tile([P, N], BF16, name=f"h_bf_{c}") for c in range(CB)]
-        for n in range(NT):
-            for c in range(CB):
-                nc.vector.tensor_copy(h_bf[c][:, chunk(n)], h_f32[c][:, chunk(n)])
+        for n in range(1, NT):
+            round_h(n)
 
         a_bf = [held.tile([P, N], BF16, name=f"a_bf_{m}") for m in range(HB)]
         t_bf = [held.tile([P, N], BF16, name=f"t_bf_{m}") for m in range(HB)]
         y = [held.tile([P, N], F32, name=f"y_{c}") for c in range(CB)]
 
         def layer1(n):
-            for m in range(HB):
-                acc = linear(nc, psum, w1_sb, h_bf, m, n)
-                nc.scalar.activation(a_bf[m][:, chunk(n)], acc[:], SILU, bias=bias_column("b1", m))
+            for m0 in range(0, HB, SIDE):
+                banks = [psum.tile([P, TOK], F32, name="acc") for m in range(SIDE)]
+                for k in range(CB):
+                    for i, acc in enumerate(banks):
+                        nc.tensor.matmul(
+                            acc[:], w1_sb[:, k, block(m0 + i)], h_bf[k][:, chunk(n)], start=(k == 0), stop=(k == CB - 1)
+                        )
+                for i, acc in enumerate(banks):
+                    nc.scalar.activation(a_bf[m0 + i][:, chunk(n)], acc[:], SILU, bias=bias_column("b1", m0 + i))
 
         def layer2(n):
             for m in range(HB):

@@ -14,7 +14,7 @@ CB = C // P
 HB = H // P
 TOK = 512
 NT = N // TOK
-SIDE = 3
+WARM = 10
 FLOPS = 2 * N * (C * H + H * H + H * C)
 
 
@@ -42,11 +42,21 @@ def tile_kanex_b_kernel(tc, base, h, w1, b1, w2, b2, w3, b3, offs, out):
         tc.tile_pool(name="held", bufs=1) as held,
         tc.psum_pool(name="psum", bufs=8) as psum,
     ):
+        zeros = held.tile([P, TOK], BF16, name="zeros")
+        nc.vector.memset(zeros[:], 0.0)
+        idle = psum.tile([P, TOK], F32, name="acc")
+        for i in range(WARM):
+            nc.tensor.matmul(idle[:], zeros[:, :P], zeros[:], start=True, stop=True)
+
         w1_sb = held.tile([P, CB, H], BF16, name="w1_sb")
+        nc.sync.dma_start(w1_sb[:], w1.rearrange("(k p) m -> p k m", p=P))
         h_f32 = [held.tile([P, N], F32, name=f"h_f32_{c}") for c in range(CB)]
-        for k in range(CB):
-            nc.scalar.dma_start(w1_sb[:, k, :], w1[block(k), :])
-            nc.sync.dma_start(h_f32[k][:, chunk(0)], h[block(k), chunk(0)])
+
+        def load_h(n):
+            for c in range(CB):
+                nc.sync.dma_start(h_f32[c][:, chunk(n)], h[block(c), chunk(n)])
+
+        load_h(0)
 
         bias_rows = held.tile([P, P], F32, name="bias_rows")
         nc.vector.memset(bias_rows[:], 0.0)
@@ -55,14 +65,13 @@ def tile_kanex_b_kernel(tc, base, h, w1, b1, w2, b2, w3, b3, offs, out):
         for name, vector in (("b1", b1), ("b2", b2), ("b3", b3)):
             rows = vector.shape[0] // P
             first_row[name] = rows_used
-            nc.scalar.dma_start(
+            nc.sync.dma_start(
                 bias_rows[rows_used : rows_used + rows, :], vector.rearrange("(m p) o -> m (p o)", p=P)
             )
             rows_used += rows
 
-        def load_h(n):
-            for c in range(CB):
-                nc.sync.dma_start(h_f32[c][:, chunk(n)], h[block(c), chunk(n)])
+        offsets = held.tile([P, N // 16], U16, name="offsets")
+        nc.sync.dma_start(offsets[:], offs)
 
         load_h(1)
         w2_sb = held.tile([P, HB, H], BF16, name="w2_sb")
@@ -71,8 +80,6 @@ def tile_kanex_b_kernel(tc, base, h, w1, b1, w2, b2, w3, b3, offs, out):
         load_h(3)
         w3_sb = held.tile([P, HB, C], BF16, name="w3_sb")
         nc.sync.dma_start(w3_sb[:], w3.rearrange("(k p) m -> p k m", p=P))
-        offsets = held.tile([P, N // 16], U16, name="offsets")
-        nc.sync.dma_start(offsets[:], offs)
         window = [held.tile([P, S], F32, name=f"window_{c}") for c in range(CB)]
         for c in range(CB):
             nc.sync.dma_start(window[c][:], base[block(c), :])
@@ -104,15 +111,9 @@ def tile_kanex_b_kernel(tc, base, h, w1, b1, w2, b2, w3, b3, offs, out):
         y = [held.tile([P, N], F32, name=f"y_{c}") for c in range(CB)]
 
         def layer1(n):
-            for m0 in range(0, HB, SIDE):
-                banks = [psum.tile([P, TOK], F32, name="acc") for m in range(SIDE)]
-                for k in range(CB):
-                    for i, acc in enumerate(banks):
-                        nc.tensor.matmul(
-                            acc[:], w1_sb[:, k, block(m0 + i)], h_bf[k][:, chunk(n)], start=(k == 0), stop=(k == CB - 1)
-                        )
-                for i, acc in enumerate(banks):
-                    nc.scalar.activation(a_bf[m0 + i][:, chunk(n)], acc[:], SILU, bias=bias_column("b1", m0 + i))
+            for m in range(HB):
+                acc = linear(nc, psum, w1_sb, h_bf, m, n)
+                nc.scalar.activation(a_bf[m][:, chunk(n)], acc[:], SILU, bias=bias_column("b1", m))
 
         def layer2(n):
             for m in range(HB):

@@ -1,5 +1,4 @@
 import concourse.mybir as mybir
-from concourse.masks import make_identity
 
 BF16 = mybir.dt.bfloat16
 F32 = mybir.dt.float32
@@ -14,7 +13,7 @@ CB = C // P
 HB = H // P
 TOK = 512
 NT = N // TOK
-WARM = 10
+WARM = 5
 FLOPS = 2 * N * (C * H + H * H + H * C)
 
 
@@ -26,12 +25,16 @@ def chunk(n):
     return slice(n * TOK, (n + 1) * TOK)
 
 
+def blocks_first(matrix):
+    return matrix.rearrange("(k p) m -> p k m", p=P)
+
+
 def linear(nc, psum, weights, moving, out_block, n):
     acc = psum.tile([P, TOK], F32, name="acc")
-    last = len(moving) - 1
-    for k, rows in enumerate(moving):
+    blocks = moving.shape[1]
+    for k in range(blocks):
         nc.tensor.matmul(
-            acc[:], weights[:, k, block(out_block)], rows[:, chunk(n)], start=(k == 0), stop=(k == last)
+            acc[:], weights[:, k, block(out_block)], moving[:, k, chunk(n)], start=(k == 0), stop=(k == blocks - 1)
         )
     return acc
 
@@ -49,82 +52,73 @@ def tile_kanex_b_kernel(tc, base, h, w1, b1, w2, b2, w3, b3, offs, out):
             nc.tensor.matmul(idle[:], zeros[:, :P], zeros[:], start=True, stop=True)
 
         w1_sb = held.tile([P, CB, H], BF16, name="w1_sb")
-        nc.sync.dma_start(w1_sb[:], w1.rearrange("(k p) m -> p k m", p=P))
-        h_f32 = [held.tile([P, N], F32, name=f"h_f32_{c}") for c in range(CB)]
+        w2_sb = held.tile([P, HB, H], BF16, name="w2_sb")
+        w3_sb = held.tile([P, HB, C], BF16, name="w3_sb")
+        h_f32 = held.tile([P, CB, N], F32, name="h_f32")
+        offsets = held.tile([P, N // 16], U16, name="offsets")
+        window = [held.tile([P, S], F32, name=f"window_{c}") for c in range(CB)]
+        bias1 = held.tile([P, HB], F32, name="bias1")
+        bias2 = held.tile([P, HB], F32, name="bias2")
+        bias3 = held.tile([P, CB], F32, name="bias3")
+
+        def load_bias(tile, vector):
+            nc.scalar.dma_start(tile[:], vector.rearrange("(m p) o -> p (m o)", p=P))
 
         def load_h(n):
-            for c in range(CB):
-                nc.sync.dma_start(h_f32[c][:, chunk(n)], h[block(c), chunk(n)])
+            nc.sync.dma_start(h_f32[:, :, chunk(n)], blocks_first(h)[:, :, chunk(n)])
 
-        load_h(0)
-
-        bias_rows = held.tile([P, P], F32, name="bias_rows")
-        nc.vector.memset(bias_rows[:], 0.0)
-        first_row = {}
-        rows_used = 0
-        for name, vector in (("b1", b1), ("b2", b2), ("b3", b3)):
-            rows = vector.shape[0] // P
-            first_row[name] = rows_used
-            nc.sync.dma_start(
-                bias_rows[rows_used : rows_used + rows, :], vector.rearrange("(m p) o -> m (p o)", p=P)
-            )
-            rows_used += rows
-
-        offsets = held.tile([P, N // 16], U16, name="offsets")
-        nc.sync.dma_start(offsets[:], offs)
-
+        for c in range(CB):
+            nc.sync.dma_start(h_f32[:, c, chunk(0)], h[block(c), chunk(0)])
+            nc.sync.dma_start(w1_sb[:, c, :], w1[block(c), :])
+        load_bias(bias1, b1)
         load_h(1)
-        w2_sb = held.tile([P, HB, H], BF16, name="w2_sb")
-        nc.sync.dma_start(w2_sb[:], w2.rearrange("(k p) m -> p k m", p=P))
+        nc.sync.dma_start(w2_sb[:], blocks_first(w2))
+        load_bias(bias2, b2)
         load_h(2)
         load_h(3)
-        w3_sb = held.tile([P, HB, C], BF16, name="w3_sb")
-        nc.sync.dma_start(w3_sb[:], w3.rearrange("(k p) m -> p k m", p=P))
-        window = [held.tile([P, S], F32, name=f"window_{c}") for c in range(CB)]
+        nc.sync.dma_start(w3_sb[:], blocks_first(w3))
+        load_bias(bias3, b3)
+        nc.sync.dma_start(offsets[:], offs)
         for c in range(CB):
             nc.sync.dma_start(window[c][:], base[block(c), :])
 
-        h_bf = [held.tile([P, N], BF16, name=f"h_bf_{c}") for c in range(CB)]
-
-        def round_h(n):
-            for c in range(CB):
-                nc.vector.tensor_copy(h_bf[c][:, chunk(n)], h_f32[c][:, chunk(n)])
-
-        round_h(0)
-
-        identity = held.tile([P, P], F32, name="identity")
-        make_identity(nc, identity[:])
-        flipped = psum.tile([P, TOK], F32, name="acc")
-        nc.tensor.transpose(flipped[:, :P], bias_rows[:], identity[:])
-        bias = held.tile([P, rows_used], F32, name="bias")
-        nc.vector.tensor_copy(bias[:], flipped[:, :rows_used])
-
-        def bias_column(name, i):
-            j = first_row[name] + i
-            return bias[:, j : j + 1]
-
+        h_bf = held.tile([P, CB, N], BF16, name="h_bf")
+        for c in range(CB):
+            nc.vector.tensor_copy(h_bf[:, c, chunk(0)], h_f32[:, c, chunk(0)])
         for n in range(1, NT):
-            round_h(n)
+            nc.vector.tensor_copy(h_bf[:, :, chunk(n)], h_f32[:, :, chunk(n)])
 
-        a_bf = [held.tile([P, N], BF16, name=f"a_bf_{m}") for m in range(HB)]
-        t_bf = [held.tile([P, N], BF16, name=f"t_bf_{m}") for m in range(HB)]
+        a_bf = held.tile([P, HB, N], BF16, name="a_bf")
+        t_bf = held.tile([P, HB, N], BF16, name="t_bf")
         y = [held.tile([P, N], F32, name=f"y_{c}") for c in range(CB)]
+
+        def silu_out(acc, m, n):
+            nc.scalar.activation(a_bf[:, m, chunk(n)], acc[:], SILU, bias=bias1[:, m : m + 1])
+
+        def layer1_as_loads_arrive(n):
+            accs = [psum.tile([P, TOK], F32, name="acc") for m in range(HB)]
+            for k in range(CB):
+                for m in range(HB):
+                    nc.tensor.matmul(
+                        accs[m][:], w1_sb[:, k, block(m)], h_bf[:, k, chunk(n)], start=(k == 0), stop=(k == CB - 1)
+                    )
+            for m in range(HB):
+                silu_out(accs[m], m, n)
 
         def layer1(n):
             for m in range(HB):
-                acc = linear(nc, psum, w1_sb, h_bf, m, n)
-                nc.scalar.activation(a_bf[m][:, chunk(n)], acc[:], SILU, bias=bias_column("b1", m))
+                silu_out(linear(nc, psum, w1_sb, h_bf, m, n), m, n)
 
         def layer2(n):
             for m in range(HB):
                 acc = linear(nc, psum, w2_sb, a_bf, m, n)
-                nc.vector.tensor_scalar_add(t_bf[m][:, chunk(n)], acc[:], bias_column("b2", m))
+                nc.vector.tensor_scalar_add(t_bf[:, m, chunk(n)], acc[:], bias2[:, m : m + 1])
 
         def layer3(c, n):
             acc = linear(nc, psum, w3_sb, t_bf, c, n)
-            nc.scalar.activation(y[c][:, chunk(n)], acc[:], IDENTITY, bias=bias_column("b3", c))
+            nc.scalar.activation(y[c][:, chunk(n)], acc[:], IDENTITY, bias=bias3[:, c : c + 1])
 
-        layer1(0)
+        layer1_as_loads_arrive(0)
         for n in range(NT):
             if n + 1 < NT:
                 layer1(n + 1)
@@ -133,5 +127,5 @@ def tile_kanex_b_kernel(tc, base, h, w1, b1, w2, b2, w3, b3, offs, out):
         for c in range(CB):
             for n in range(NT):
                 layer3(c, n)
-            nc.vector.tensor_tensor(window[c][:].indirect(offsets[:]), y[c][:], h_f32[c][:], ADD)
+            nc.vector.tensor_tensor(window[c][:].indirect(offsets[:]), y[c][:], h_f32[:, c, :], ADD)
             nc.sync.dma_start(out[block(c), :], window[c][:])

@@ -1,4 +1,5 @@
 import concourse.mybir as mybir
+from concourse.masks import make_identity
 
 BF16 = mybir.dt.bfloat16
 F32 = mybir.dt.float32
@@ -57,12 +58,28 @@ def tile_kanex_b_kernel(tc, base, h, w1, b1, w2, b2, w3, b3, offs, out):
         h_f32 = held.tile([P, CB, N], F32, name="h_f32")
         offsets = held.tile([P, N // 16], U16, name="offsets")
         window = [held.tile([P, S], F32, name=f"window_{c}") for c in range(CB)]
-        bias1 = held.tile([P, HB], F32, name="bias1")
-        bias2 = held.tile([P, HB], F32, name="bias2")
-        bias3 = held.tile([P, CB], F32, name="bias3")
 
-        def load_bias(tile, vector):
-            nc.scalar.dma_start(tile[:], vector.rearrange("(m p) o -> p (m o)", p=P))
+        bias_rows = held.tile([P, P], F32, name="bias_rows")
+        nc.gpsimd.memset(bias_rows[:], 0.0)
+        identity = held.tile([P, P], F32, name="identity")
+        make_identity(nc, identity[:])
+        first_row = {"b1": 0, "b2": HB, "b3": 2 * HB}
+        rows_used = 2 * HB + CB
+        bias = held.tile([P, rows_used], F32, name="bias")
+
+        def load_bias_rows():
+            for name, vector in (("b1", b1), ("b2", b2), ("b3", b3)):
+                rows = slice(first_row[name], first_row[name] + vector.shape[0] // P)
+                nc.scalar.dma_start(bias_rows[rows, :], vector.rearrange("(m p) o -> m (p o)", p=P))
+
+        def flip_biases():
+            flipped = psum.tile([P, TOK], F32, name="acc")
+            nc.tensor.transpose(flipped[:, :P], bias_rows[:], identity[:])
+            nc.vector.tensor_copy(bias[:], flipped[:, :rows_used])
+
+        def bias_column(name, i):
+            j = first_row[name] + i
+            return bias[:, j : j + 1]
 
         def load_h(n):
             nc.sync.dma_start(h_f32[:, :, chunk(n)], blocks_first(h)[:, :, chunk(n)])
@@ -70,14 +87,12 @@ def tile_kanex_b_kernel(tc, base, h, w1, b1, w2, b2, w3, b3, offs, out):
         for c in range(CB):
             nc.sync.dma_start(h_f32[:, c, chunk(0)], h[block(c), chunk(0)])
             nc.sync.dma_start(w1_sb[:, c, :], w1[block(c), :])
-        load_bias(bias1, b1)
         load_h(1)
+        load_bias_rows()
         nc.sync.dma_start(w2_sb[:], blocks_first(w2))
-        load_bias(bias2, b2)
         load_h(2)
         load_h(3)
         nc.sync.dma_start(w3_sb[:], blocks_first(w3))
-        load_bias(bias3, b3)
         nc.sync.dma_start(offsets[:], offs)
         for c in range(CB):
             nc.sync.dma_start(window[c][:], base[block(c), :])
@@ -93,7 +108,7 @@ def tile_kanex_b_kernel(tc, base, h, w1, b1, w2, b2, w3, b3, offs, out):
         y = [held.tile([P, N], F32, name=f"y_{c}") for c in range(CB)]
 
         def silu_out(acc, m, n):
-            nc.scalar.activation(a_bf[:, m, chunk(n)], acc[:], SILU, bias=bias1[:, m : m + 1])
+            nc.scalar.activation(a_bf[:, m, chunk(n)], acc[:], SILU, bias=bias_column("b1", m))
 
         def layer1_as_loads_arrive(n):
             accs = [psum.tile([P, TOK], F32, name="acc") for m in range(HB)]
@@ -102,6 +117,8 @@ def tile_kanex_b_kernel(tc, base, h, w1, b1, w2, b2, w3, b3, offs, out):
                     nc.tensor.matmul(
                         accs[m][:], w1_sb[:, k, block(m)], h_bf[:, k, chunk(n)], start=(k == 0), stop=(k == CB - 1)
                     )
+                if k == CB - 2:
+                    flip_biases()
             for m in range(HB):
                 silu_out(accs[m], m, n)
 
@@ -112,11 +129,11 @@ def tile_kanex_b_kernel(tc, base, h, w1, b1, w2, b2, w3, b3, offs, out):
         def layer2(n):
             for m in range(HB):
                 acc = linear(nc, psum, w2_sb, a_bf, m, n)
-                nc.vector.tensor_scalar_add(t_bf[:, m, chunk(n)], acc[:], bias2[:, m : m + 1])
+                nc.vector.tensor_scalar_add(t_bf[:, m, chunk(n)], acc[:], bias_column("b2", m))
 
         def layer3(c, n):
             acc = linear(nc, psum, w3_sb, t_bf, c, n)
-            nc.scalar.activation(y[c][:, chunk(n)], acc[:], IDENTITY, bias=bias3[:, c : c + 1])
+            nc.scalar.activation(y[c][:, chunk(n)], acc[:], IDENTITY, bias=bias_column("b3", c))
 
         layer1_as_loads_arrive(0)
         for n in range(NT):

@@ -59,27 +59,28 @@ def tile_kanex_b_kernel(tc, base, h, w1, b1, w2, b2, w3, b3, offs, out):
         offsets = held.tile([P, N // 16], U16, name="offsets")
         window = [held.tile([P, S], F32, name=f"window_{c}") for c in range(CB)]
 
-        bias_rows = held.tile([P, P], F32, name="bias_rows")
+        bias_rows = held.tile([P, C], F32, name="bias_rows")
         nc.gpsimd.memset(bias_rows[:], 0.0)
         identity = held.tile([P, P], F32, name="identity")
         make_identity(nc, identity[:])
-        first_row = {"b1": 0, "b2": HB, "b3": 2 * HB}
-        rows_used = 2 * HB + CB
-        bias = held.tile([P, rows_used], F32, name="bias")
+        first_row = {"b1": 0, "b2": H // C, "b3": 2 * (H // C)}
+        rows_used = 2 * (H // C) + 1
+        bias = held.tile([P, CB, rows_used], F32, name="bias")
 
         def load_bias_rows():
             for name, vector in (("b1", b1), ("b2", b2), ("b3", b3)):
-                rows = slice(first_row[name], first_row[name] + vector.shape[0] // P)
-                nc.scalar.dma_start(bias_rows[rows, :], vector.rearrange("(m p) o -> m (p o)", p=P))
+                rows = slice(first_row[name], first_row[name] + vector.shape[0] // C)
+                nc.sync.dma_start(bias_rows[rows, :], vector.rearrange("(r q) o -> r (q o)", q=C))
 
         def flip_biases():
             flipped = psum.tile([P, TOK], F32, name="acc")
-            nc.tensor.transpose(flipped[:, :P], bias_rows[:], identity[:])
-            nc.vector.tensor_copy(bias[:], flipped[:, :rows_used])
+            for j in range(CB):
+                nc.tensor.transpose(flipped[:, block(j)], bias_rows[:, block(j)], identity[:])
+            for j in range(CB):
+                nc.vector.tensor_copy(bias[:, j, :], flipped[:, j * P : j * P + rows_used])
 
         def bias_column(name, i):
-            j = first_row[name] + i
-            return bias[:, j : j + 1]
+            return bias[:, i % CB, first_row[name] + i // CB : first_row[name] + i // CB + 1]
 
         def load_h(n):
             nc.sync.dma_start(h_f32[:, :, chunk(n)], blocks_first(h)[:, :, chunk(n)])
@@ -87,8 +88,9 @@ def tile_kanex_b_kernel(tc, base, h, w1, b1, w2, b2, w3, b3, offs, out):
         for c in range(CB):
             nc.sync.dma_start(h_f32[:, c, chunk(0)], h[block(c), chunk(0)])
             nc.sync.dma_start(w1_sb[:, c, :], w1[block(c), :])
+            if c == 0:
+                load_bias_rows()
         load_h(1)
-        load_bias_rows()
         nc.sync.dma_start(w2_sb[:], blocks_first(w2))
         load_h(2)
         load_h(3)
@@ -117,7 +119,7 @@ def tile_kanex_b_kernel(tc, base, h, w1, b1, w2, b2, w3, b3, offs, out):
                     nc.tensor.matmul(
                         accs[m][:], w1_sb[:, k, block(m)], h_bf[:, k, chunk(n)], start=(k == 0), stop=(k == CB - 1)
                     )
-                if k == CB - 2:
+                if k == 0:
                     flip_biases()
             for m in range(HB):
                 silu_out(accs[m], m, n)

@@ -1,5 +1,4 @@
 import concourse.mybir as mybir
-from concourse.masks import make_identity
 
 BF16 = mybir.dt.bfloat16
 F32 = mybir.dt.float32
@@ -14,7 +13,10 @@ CB = C // P
 HB = H // P
 TOK = 512
 NT = N // TOK
-WARM = 5
+SQUARE = 32
+BLOCK_COLS = 256
+WARM_COLS = 256
+WARM = 8
 FLOPS = 2 * N * (C * H + H * H + H * C)
 
 
@@ -24,6 +26,10 @@ def block(i):
 
 def chunk(n):
     return slice(n * TOK, (n + 1) * TOK)
+
+
+def half_of(width, i):
+    return slice(i * width // 2, (i + 1) * width // 2)
 
 
 def blocks_first(matrix):
@@ -46,11 +52,11 @@ def tile_kanex_b_kernel(tc, base, h, w1, b1, w2, b2, w3, b3, offs, out):
         tc.tile_pool(name="held", bufs=1) as held,
         tc.psum_pool(name="psum", bufs=8) as psum,
     ):
-        zeros = held.tile([P, TOK], BF16, name="zeros")
-        nc.vector.memset(zeros[:], 0.0)
+        zeros = held.tile([P, WARM_COLS], BF16, name="zeros")
+        nc.gpsimd.memset(zeros[:], 0.0)
         idle = psum.tile([P, TOK], F32, name="acc")
         for i in range(WARM):
-            nc.tensor.matmul(idle[:], zeros[:, :P], zeros[:], start=True, stop=True)
+            nc.tensor.matmul(idle[:, :WARM_COLS], zeros[:, :P], zeros[:], start=True, stop=True)
 
         w1_sb = held.tile([P, CB, H], BF16, name="w1_sb")
         w2_sb = held.tile([P, HB, H], BF16, name="w2_sb")
@@ -59,37 +65,31 @@ def tile_kanex_b_kernel(tc, base, h, w1, b1, w2, b2, w3, b3, offs, out):
         offsets = held.tile([P, N // 16], U16, name="offsets")
         window = [held.tile([P, S], F32, name=f"window_{c}") for c in range(CB)]
 
-        bias_rows = held.tile([P, C], F32, name="bias_rows")
+        bias_rows = held.tile([P, BLOCK_COLS], F32, name="bias_rows", align_bytes=64)
         nc.gpsimd.memset(bias_rows[:], 0.0)
-        identity = held.tile([P, P], F32, name="identity")
-        make_identity(nc, identity[:])
-        first_row = {"b1": 0, "b2": H // C, "b3": 2 * (H // C)}
-        rows_used = 2 * (H // C) + 1
-        bias = held.tile([P, CB, rows_used], F32, name="bias")
+        bias = held.tile([P, BLOCK_COLS], F32, name="bias", align_bytes=64)
+        bias_row = {"b1": 0, "b2": 1, "b3": 2}
 
         def load_bias_rows():
             for name, vector in (("b1", b1), ("b2", b2), ("b3", b3)):
-                rows = slice(first_row[name], first_row[name] + vector.shape[0] // C)
-                nc.sync.dma_start(bias_rows[rows, :], vector.rearrange("(r q) o -> r (q o)", q=C))
-
-        def flip_biases():
-            flipped = psum.tile([P, TOK], F32, name="acc")
-            for j in range(CB):
-                nc.tensor.transpose(flipped[:, block(j)], bias_rows[:, block(j)], identity[:])
-            for j in range(CB):
-                nc.vector.tensor_copy(bias[:, j, :], flipped[:, j * P : j * P + rows_used])
+                pieces = vector.rearrange("(i q s) o -> q i (s o)", q=P // SQUARE, s=SQUARE)
+                rows = bias_rows[bias_row[name] : P : SQUARE, : vector.shape[0] // (P // SQUARE)]
+                nc.sync.dma_start(rows.rearrange("q (i s) -> q i s", s=SQUARE), pieces)
 
         def bias_column(name, i):
-            return bias[:, i % CB, first_row[name] + i // CB : first_row[name] + i // CB + 1]
+            column = SQUARE * i + bias_row[name]
+            return bias[:, column : column + 1]
 
         def load_h(n):
             nc.sync.dma_start(h_f32[:, :, chunk(n)], blocks_first(h)[:, :, chunk(n)])
 
-        for c in range(CB):
+        for half in range(2):
+            nc.sync.dma_start(h_f32[:, 0, half_of(TOK, half)], h[block(0), half_of(TOK, half)])
+            nc.sync.dma_start(w1_sb[:, 0, half_of(H, half)], w1[block(0), half_of(H, half)])
+        for c in range(1, CB):
             nc.sync.dma_start(h_f32[:, c, chunk(0)], h[block(c), chunk(0)])
             nc.sync.dma_start(w1_sb[:, c, :], w1[block(c), :])
-            if c == 0:
-                load_bias_rows()
+        load_bias_rows()
         load_h(1)
         nc.sync.dma_start(w2_sb[:], blocks_first(w2))
         load_h(2)
@@ -100,8 +100,11 @@ def tile_kanex_b_kernel(tc, base, h, w1, b1, w2, b2, w3, b3, offs, out):
             nc.sync.dma_start(window[c][:], base[block(c), :])
 
         h_bf = held.tile([P, CB, N], BF16, name="h_bf")
-        for c in range(CB):
+        for half in range(2):
+            nc.vector.tensor_copy(h_bf[:, 0, half_of(TOK, half)], h_f32[:, 0, half_of(TOK, half)])
+        for c in range(1, CB):
             nc.vector.tensor_copy(h_bf[:, c, chunk(0)], h_f32[:, c, chunk(0)])
+        nc.vector.transpose(bias[:], bias_rows[:])
         for n in range(1, NT):
             nc.vector.tensor_copy(h_bf[:, :, chunk(n)], h_f32[:, :, chunk(n)])
 
@@ -119,8 +122,6 @@ def tile_kanex_b_kernel(tc, base, h, w1, b1, w2, b2, w3, b3, offs, out):
                     nc.tensor.matmul(
                         accs[m][:], w1_sb[:, k, block(m)], h_bf[:, k, chunk(n)], start=(k == 0), stop=(k == CB - 1)
                     )
-                if k == 0:
-                    flip_biases()
             for m in range(HB):
                 silu_out(accs[m], m, n)
 

@@ -36,14 +36,15 @@ def blocks_first(matrix):
     return matrix.rearrange("(k p) m -> p k m", p=P)
 
 
-def linear(nc, psum, weights, moving, out_block, n):
+def linear(nc, psum, weights, moving, out_block, tokens):
     acc = psum.tile([P, TOK], F32, name="acc")
+    product = acc[:, : tokens.stop - tokens.start]
     blocks = moving.shape[1]
     for k in range(blocks):
         nc.tensor.matmul(
-            acc[:], weights[:, k, block(out_block)], moving[:, k, chunk(n)], start=(k == 0), stop=(k == blocks - 1)
+            product, weights[:, k, block(out_block)], moving[:, k, tokens], start=(k == 0), stop=(k == blocks - 1)
         )
-    return acc
+    return product
 
 
 def tile_kanex_b_kernel(tc, base, h, w1, b1, w2, b2, w3, b3, offs, out):
@@ -113,7 +114,7 @@ def tile_kanex_b_kernel(tc, base, h, w1, b1, w2, b2, w3, b3, offs, out):
         y = [held.tile([P, N], F32, name=f"y_{c}") for c in range(CB)]
 
         def silu_out(acc, m, n):
-            nc.scalar.activation(a_bf[:, m, chunk(n)], acc[:], SILU, bias=bias_column("b1", m))
+            nc.scalar.activation(a_bf[:, m, chunk(n)], acc, SILU, bias=bias_column("b1", m))
 
         def layer1_as_loads_arrive(n):
             accs = [psum.tile([P, TOK], F32, name="acc") for m in range(HB)]
@@ -123,20 +124,23 @@ def tile_kanex_b_kernel(tc, base, h, w1, b1, w2, b2, w3, b3, offs, out):
                         accs[m][:], w1_sb[:, k, block(m)], h_bf[:, k, chunk(n)], start=(k == 0), stop=(k == CB - 1)
                     )
             for m in range(HB):
-                silu_out(accs[m], m, n)
+                silu_out(accs[m][:], m, n)
 
         def layer1(n):
             for m in range(HB):
-                silu_out(linear(nc, psum, w1_sb, h_bf, m, n), m, n)
+                silu_out(linear(nc, psum, w1_sb, h_bf, m, chunk(n)), m, n)
 
         def layer2(n):
             for m in range(HB):
-                acc = linear(nc, psum, w2_sb, a_bf, m, n)
-                nc.vector.tensor_scalar_add(t_bf[:, m, chunk(n)], acc[:], bias_column("b2", m))
+                acc = linear(nc, psum, w2_sb, a_bf, m, chunk(n))
+                nc.vector.tensor_scalar_add(t_bf[:, m, chunk(n)], acc, bias_column("b2", m))
 
-        def layer3(c, n):
-            acc = linear(nc, psum, w3_sb, t_bf, c, n)
-            nc.scalar.activation(y[c][:, chunk(n)], acc[:], IDENTITY, bias=bias_column("b3", c))
+        def layer3(c, tokens):
+            acc = linear(nc, psum, w3_sb, t_bf, c, tokens)
+            if c == 0:
+                nc.vector.tensor_scalar_add(y[c][:, tokens], acc, bias_column("b3", c))
+            else:
+                nc.scalar.activation(y[c][:, tokens], acc, IDENTITY, bias=bias_column("b3", c))
 
         layer1_as_loads_arrive(0)
         for n in range(NT):
@@ -144,8 +148,9 @@ def tile_kanex_b_kernel(tc, base, h, w1, b1, w2, b2, w3, b3, offs, out):
                 layer1(n + 1)
             layer2(n)
 
+        last_in_halves = [chunk(n) for n in range(NT - 1)] + [slice(N - TOK, N - TOK // 2), slice(N - TOK // 2, N)]
         for c in range(CB):
-            for n in range(NT):
-                layer3(c, n)
+            for tokens in last_in_halves if c == 0 else map(chunk, range(NT)):
+                layer3(c, tokens)
             nc.vector.tensor_tensor(window[c][:].indirect(offsets[:]), y[c][:], h_f32[:, c, :], ADD)
             nc.sync.dma_start(out[block(c), :], window[c][:])

@@ -86,6 +86,7 @@ def tile_kanex_b_kernel(tc, base, h, w1, b1, w2, b2, w3, b3, offs, out):
 
         for half in range(2):
             nc.sync.dma_start(h_f32[:, 0, half_of(TOK, half)], h[block(0), half_of(TOK, half)])
+        for half in range(2):
             nc.sync.dma_start(w1_sb[:, 0, half_of(H, half)], w1[block(0), half_of(H, half)])
         for c in range(1, CB):
             nc.sync.dma_start(h_f32[:, c, chunk(0)], h[block(c), chunk(0)])

@@ -92,7 +92,8 @@ def tile_kanex_b_kernel(tc, base, h, w1, b1, w2, b2, w3, b3, offs, out):
             nc.sync.dma_start(h_f32[:, c, chunk(0)], h[block(c), chunk(0)])
             nc.sync.dma_start(w1_sb[:, c, :], w1[block(c), :])
         load_bias_rows()
-        load_h(1)
+        for c in range(CB):
+            nc.sync.dma_start(h_f32[:, c, chunk(1)], h[block(c), chunk(1)])
         nc.sync.dma_start(w2_sb[:], blocks_first(w2))
         load_h(2)
         load_h(3)
@@ -107,7 +108,9 @@ def tile_kanex_b_kernel(tc, base, h, w1, b1, w2, b2, w3, b3, offs, out):
         for c in range(1, CB):
             nc.vector.tensor_copy(h_bf[:, c, chunk(0)], h_f32[:, c, chunk(0)])
         nc.vector.transpose(bias[:], bias_rows[:])
-        for n in range(1, NT):
+        for c in range(CB):
+            nc.vector.tensor_copy(h_bf[:, c, chunk(1)], h_f32[:, c, chunk(1)])
+        for n in range(2, NT):
             nc.vector.tensor_copy(h_bf[:, :, chunk(n)], h_f32[:, :, chunk(n)])
 
         a_bf = held.tile([P, HB, N], BF16, name="a_bf")

@@ -59,6 +59,9 @@ def tile_kanex_b_kernel(tc, base, h, w1, b1, w2, b2, w3, b3, offs, out):
         for i in range(WARM):
             nc.tensor.matmul(idle[:, :WARM_COLS], zeros[:, :P], zeros[:], start=True, stop=True)
 
+        silu_of_zero = held.tile([P, 1], BF16, name="silu_of_zero")
+        nc.scalar.activation(silu_of_zero[:], zeros[:, :1], SILU)
+
         w1_sb = held.tile([P, CB, H], BF16, name="w1_sb")
         w2_sb = held.tile([P, HB, H], BF16, name="w2_sb")
         w3_sb = held.tile([P, HB, C], BF16, name="w3_sb")
@@ -152,9 +155,12 @@ def tile_kanex_b_kernel(tc, base, h, w1, b1, w2, b2, w3, b3, offs, out):
                 layer1(n + 1)
             layer2(n)
 
-        last_in_halves = [chunk(n) for n in range(NT - 1)] + [slice(N - TOK, N - TOK // 2), slice(N - TOK // 2, N)]
+        tail = N - TOK
+        pieces_of_block_0 = [chunk(n) for n in range(NT - 1)] + [
+            slice(tail, tail + TOK // 2), slice(tail + TOK // 2, N - TOK // 4), slice(N - TOK // 4, N)
+        ]
         for c in range(CB):
-            for tokens in last_in_halves if c == 0 else map(chunk, range(NT)):
+            for tokens in pieces_of_block_0 if c == 0 else map(chunk, range(NT)):
                 layer3(c, tokens)
             nc.vector.tensor_tensor(window[c][:].indirect(offsets[:]), y[c][:], h_f32[:, c, :], ADD)
             nc.sync.dma_start(out[block(c), :], window[c][:])

@@ -59,9 +59,6 @@ def tile_kanex_b_kernel(tc, base, h, w1, b1, w2, b2, w3, b3, offs, out):
         for i in range(WARM):
             nc.tensor.matmul(idle[:, :WARM_COLS], zeros[:, :P], zeros[:], start=True, stop=True)
 
-        silu_of_zero = held.tile([P, 1], BF16, name="silu_of_zero")
-        nc.scalar.activation(silu_of_zero[:], zeros[:, :1], SILU)
-
         w1_sb = held.tile([P, CB, H], BF16, name="w1_sb")
         w2_sb = held.tile([P, HB, H], BF16, name="w2_sb")
         w3_sb = held.tile([P, HB, C], BF16, name="w3_sb")
@@ -84,9 +81,6 @@ def tile_kanex_b_kernel(tc, base, h, w1, b1, w2, b2, w3, b3, offs, out):
             column = SQUARE * i + bias_row[name]
             return bias[:, column : column + 1]
 
-        def load_h(n):
-            nc.sync.dma_start(h_f32[:, :, chunk(n)], blocks_first(h)[:, :, chunk(n)])
-
         for half in range(2):
             nc.sync.dma_start(h_f32[:, 0, half_of(TOK, half)], h[block(0), half_of(TOK, half)])
         for half in range(2):
@@ -98,8 +92,7 @@ def tile_kanex_b_kernel(tc, base, h, w1, b1, w2, b2, w3, b3, offs, out):
         for c in range(CB):
             nc.sync.dma_start(h_f32[:, c, chunk(1)], h[block(c), chunk(1)])
         nc.sync.dma_start(w2_sb[:], blocks_first(w2))
-        load_h(2)
-        load_h(3)
+        nc.sync.dma_start(h_f32[:, :, 2 * TOK :], blocks_first(h)[:, :, 2 * TOK :])
         nc.sync.dma_start(w3_sb[:], blocks_first(w3))
         nc.sync.dma_start(offsets[:], offs)
         for c in range(CB):

import concourse.mybir as mybir

BF16 = mybir.dt.bfloat16
F32 = mybir.dt.float32
U16 = mybir.dt.uint16
ADD = mybir.AluOpType.add
SILU = mybir.ActivationFunctionType.Silu
IDENTITY = mybir.ActivationFunctionType.Identity

P = 128
C, H, S, N = 384, 768, 4096, 2048
CB = C // P
HB = H // P
TOK = 512
NT = N // TOK
SQUARE = 32
BLOCK_COLS = 256
WARM_COLS = 256
WARM = 8
FLOPS = 2 * N * (C * H + H * H + H * C)


def block(i):
    return slice(i * P, (i + 1) * P)


def chunk(n):
    return slice(n * TOK, (n + 1) * TOK)


def half_of(width, i):
    return slice(i * width // 2, (i + 1) * width // 2)


def blocks_first(matrix):
    return matrix.rearrange("(k p) m -> p k m", p=P)


def linear(nc, psum, weights, moving, out_block, tokens):
    acc = psum.tile([P, TOK], F32, name="acc")
    product = acc[:, : tokens.stop - tokens.start]
    blocks = moving.shape[1]
    for k in range(blocks):
        nc.tensor.matmul(
            product, weights[:, k, block(out_block)], moving[:, k, tokens], start=(k == 0), stop=(k == blocks - 1)
        )
    return product


def tile_kanex_b_kernel(tc, base, h, w1, b1, w2, b2, w3, b3, offs, out):
    nc = tc.nc
    with (
        tc.tile_pool(name="held", bufs=1) as held,
        tc.psum_pool(name="psum", bufs=8) as psum,
    ):
        zeros = held.tile([P, WARM_COLS], BF16, name="zeros")
        nc.gpsimd.memset(zeros[:], 0.0)
        idle = psum.tile([P, TOK], F32, name="acc")
        for i in range(WARM):
            nc.tensor.matmul(idle[:, :WARM_COLS], zeros[:, :P], zeros[:], start=True, stop=True)

        w1_sb = held.tile([P, CB, H], BF16, name="w1_sb")
        w2_sb = held.tile([P, HB, H], BF16, name="w2_sb")
        w3_sb = held.tile([P, HB, C], BF16, name="w3_sb")
        h_f32 = held.tile([P, CB, N], F32, name="h_f32")
        offsets = held.tile([P, N // 16], U16, name="offsets")
        window = [held.tile([P, S], F32, name=f"window_{c}") for c in range(CB)]

        bias_rows = held.tile([P, BLOCK_COLS], F32, name="bias_rows", align_bytes=64)
        nc.gpsimd.memset(bias_rows[:], 0.0)
        bias = held.tile([P, BLOCK_COLS], F32, name="bias", align_bytes=64)
        bias_row = {"b1": 0, "b2": 1, "b3": 2}

        def load_bias_rows():
            for name, vector in (("b1", b1), ("b2", b2), ("b3", b3)):
                pieces = vector.rearrange("(i q s) o -> q i (s o)", q=P // SQUARE, s=SQUARE)
                rows = bias_rows[bias_row[name] : P : SQUARE, : vector.shape[0] // (P // SQUARE)]
                nc.sync.dma_start(rows.rearrange("q (i s) -> q i s", s=SQUARE), pieces)

        def bias_column(name, i):
            column = SQUARE * i + bias_row[name]
            return bias[:, column : column + 1]

        for half in range(2):
            nc.sync.dma_start(h_f32[:, 0, half_of(TOK, half)], h[block(0), half_of(TOK, half)])
        for half in range(2):
            nc.sync.dma_start(w1_sb[:, 0, half_of(H, half)], w1[block(0), half_of(H, half)])
        for c in range(1, CB):
            nc.sync.dma_start(h_f32[:, c, chunk(0)], h[block(c), chunk(0)])
            nc.sync.dma_start(w1_sb[:, c, :], w1[block(c), :])
        load_bias_rows()
        for c in range(CB):
            nc.sync.dma_start(h_f32[:, c, chunk(1)], h[block(c), chunk(1)])
        nc.sync.dma_start(w2_sb[:], blocks_first(w2))
        nc.sync.dma_start(h_f32[:, :, 2 * TOK :], blocks_first(h)[:, :, 2 * TOK :])
        nc.sync.dma_start(w3_sb[:], blocks_first(w3))
        nc.sync.dma_start(offsets[:], offs)
        for c in range(CB):
            nc.sync.dma_start(window[c][:], base[block(c), :])

        h_bf = held.tile([P, CB, N], BF16, name="h_bf")
        for half in range(2):
            nc.vector.tensor_copy(h_bf[:, 0, half_of(TOK, half)], h_f32[:, 0, half_of(TOK, half)])
        for c in range(1, CB):
            nc.vector.tensor_copy(h_bf[:, c, chunk(0)], h_f32[:, c, chunk(0)])
        nc.vector.transpose(bias[:], bias_rows[:])
        for c in range(CB):
            nc.vector.tensor_copy(h_bf[:, c, chunk(1)], h_f32[:, c, chunk(1)])
        for n in range(2, NT):
            nc.vector.tensor_copy(h_bf[:, :, chunk(n)], h_f32[:, :, chunk(n)])

        a_bf = held.tile([P, HB, N], BF16, name="a_bf")
        t_bf = held.tile([P, HB, N], BF16, name="t_bf")
        y = [held.tile([P, N], F32, name=f"y_{c}") for c in range(CB)]

        def silu_out(acc, m, n):
            nc.scalar.activation(a_bf[:, m, chunk(n)], acc, SILU, bias=bias_column("b1", m))

        def layer1_as_loads_arrive(n):
            accs = [psum.tile([P, TOK], F32, name="acc") for m in range(HB)]
            for k in range(CB):
                for m in range(HB):
                    nc.tensor.matmul(
                        accs[m][:], w1_sb[:, k, block(m)], h_bf[:, k, chunk(n)], start=(k == 0), stop=(k == CB - 1)
                    )
            for m in range(HB):
                silu_out(accs[m][:], m, n)

        def layer1(n):
            for m in range(HB):
                silu_out(linear(nc, psum, w1_sb, h_bf, m, chunk(n)), m, n)

        def layer2(n):
            for m in range(HB):
                acc = linear(nc, psum, w2_sb, a_bf, m, chunk(n))
                nc.vector.tensor_scalar_add(t_bf[:, m, chunk(n)], acc, bias_column("b2", m))

        def layer3(c, tokens):
            acc = linear(nc, psum, w3_sb, t_bf, c, tokens)
            if c == 0:
                nc.vector.tensor_scalar_add(y[c][:, tokens], acc, bias_column("b3", c))
            else:
                nc.scalar.activation(y[c][:, tokens], acc, IDENTITY, bias=bias_column("b3", c))

        layer1_as_loads_arrive(0)
        for n in range(NT):
            if n + 1 < NT:
                layer1(n + 1)
            layer2(n)

        tail = N - TOK
        pieces_of_block_0 = [chunk(n) for n in range(NT - 1)] + [
            slice(tail, tail + TOK // 2), slice(tail + TOK // 2, N - TOK // 4), slice(N - TOK // 4, N)
        ]
        for c in range(CB):
            for tokens in pieces_of_block_0 if c == 0 else map(chunk, range(NT)):
                layer3(c, tokens)
            nc.vector.tensor_tensor(window[c][:].indirect(offsets[:]), y[c][:], h_f32[:, c, :], ADD)
            nc.sync.dma_start(out[block(c), :], window[c][:])
